import numpy as np
import ml_dtypes


def mxq(x, axis, fmt="e4m3"):
    dtype, down = {"e4m3": (ml_dtypes.float8_e4m3fn, 7), "e5m2": (ml_dtypes.float8_e5m2, 14)}[fmt]
    v = np.moveaxis(np.asarray(x, np.float32).astype(ml_dtypes.bfloat16).astype(np.float64), axis, -1)
    blocks = v.reshape(v.shape[:-1] + (-1, 32))
    amax = np.abs(blocks).max(-1, keepdims=True)
    byte = np.maximum(np.where(amax > 0, np.frexp(amax)[1] - 1 + 127, 0) - down, 1)
    scale = np.exp2(byte - 127.0)
    codes = (blocks / scale).astype(np.float32).astype(dtype).astype(np.float64)
    return np.moveaxis((codes * scale).reshape(v.shape), -1, axis)


WIDE = False


def mx_kscale(k):
    if not WIDE:
        return np.ones(k)
    levels = np.array([10, -10, 5, -5, 0])
    a = np.random.permutation(np.resize(levels, k // 512 * 4)).reshape(k // 512, 4)
    idx = np.arange(k)
    return np.exp2(a[idx // 512, idx % 128 // 32])


BF16 = ml_dtypes.bfloat16


def bf(x):
    return np.asarray(x, np.float32).astype(BF16)


def f64(x):
    return np.asarray(x).astype(np.float64)


B, S, H = 4, 1536, 512
M = B * S


def setup_inputs():
    s = mx_kscale(H)
    return {"x": bf(np.random.standard_normal((B, S, H)) * s),
            "plastic_weights": bf(np.random.standard_normal((H, H)) / np.sqrt(H) / s[None, :]),
            "plasticity_rate": bf(np.random.uniform(0.2, 0.4, 1)),
            "fixed_w": bf(np.random.standard_normal((H, H)) / np.sqrt(H) / s[None, :]),
            "fixed_b": bf(np.random.standard_normal(H) * 0.3),
            "hebbian_strength": bf(np.random.uniform(1.5, 2.5, 1))}


def reference(x, plastic_weights, plasticity_rate, fixed_w, fixed_b, hebbian_strength):
    xf = f64(x)
    pw = f64(plastic_weights)
    xq = mxq(xf, 2, "e4m3")
    fixed_out = (xq @ mxq(f64(fixed_w), 1, "e4m3").T) + f64(fixed_b)
    plastic_out = xq @ mxq(pw, 1, "e4m3").T
    combined = fixed_out + plastic_out
    pre = mxq(xf.reshape(M, H), 0, "e4m3")
    post = mxq(combined.reshape(M, H), 0, "e4m3")
    hebb = (pre.T @ post) / M
    plasticity_factor = f64(plasticity_rate)[0] * f64(hebbian_strength)
    new_w = pw + plasticity_factor * hebb
    w_norm = np.sqrt(np.sum(new_w ** 2))
    new_w = np.where(w_norm > 1.0, new_w / w_norm, new_w)
    return combined, new_w

@@ -1,0 +1,515 @@
+from contextlib import ExitStack
+
+import concourse.mybir as mybir
+from concourse.masks import make_identity
+
+F32 = mybir.dt.float32
+BF16 = mybir.dt.bfloat16
+U32 = mybir.dt.uint32
+U8 = mybir.dt.uint8
+FP8X4 = mybir.dt.float8_e4m3fn_x4
+ALU = mybir.AluOpType
+ACT = mybir.ActivationFunctionType
+
+P = 128
+H = 512
+ROWS = 6144
+PACK = 4
+BLK = P * PACK
+NB = ROWS // BLK
+FLOPS = 3 * 2 * ROWS * H * H
+PS_BUFS = 2
+TP_BUFS = 2
+
+
+def tile_neuroplasticitylayer_t_kernel(
+    tc, x, plastic_weights, plasticity_rate, fixed_w, fixed_b, hebbian_strength, out_0, out_1
+):
+    nc = tc.nc
+    xf = x.flatten_outer_dims()
+    of = out_0.flatten_outer_dims()
+
+    with ExitStack() as ctx:
+        ctx.enter_context(tc.manual_schedule())
+        const = ctx.enter_context(tc.tile_pool(name="const", bufs=1))
+        xpool = ctx.enter_context(tc.tile_pool(name="xpool", bufs=1))
+        work = ctx.enter_context(tc.tile_pool(name="work", bufs=2))
+        psum = ctx.enter_context(tc.psum_pool(name="psum", bufs=1))
+
+        zb = const.tile([P, 544], BF16, name="zb")
+        nc.vector.memset(zb[:], 0.0)
+        warm = const.tile([P, 1], F32, name="warm")
+        nc.vector.memset(warm[:], 1.0)
+        nc.scalar.activation(out=warm[:], in_=warm[:], func=ACT.Abs_reciprocal_sqrt)
+        ones_b = const.tile([P, P], BF16, name="ones_b")
+        nc.vector.memset(ones_b[:], 1.0)
+        ones_f = const.tile([P, P], F32, name="ones_f")
+        nc.vector.memset(ones_f[:], 1.0)
+        ident = const.tile([P, P], F32, name="ident")
+        make_identity(nc, ident[:])
+
+        raw = {}
+        raw["f"] = const.tile([P, PACK * H], BF16, name="wf_raw")
+        raw["p"] = const.tile([P, PACK * H], BF16, name="wp_raw")
+        for c in range(NB):
+            raw[c] = xpool.tile([P, PACK * H], BF16, name="x_sb%d" % c)
+        w_dram = {"f": fixed_w, "p": plastic_weights}
+
+        def load(key):
+            if key == "b":
+                nc.sync.dma_start(out=zb[0:1, 0:H], in_=fixed_b.unsqueeze(0))
+            elif key == "r":
+                nc.sync.dma_start(out=zb[0:1, 512:513], in_=plasticity_rate.unsqueeze(0))
+                nc.sync.dma_start(out=zb[0:1, 528:529], in_=hebbian_strength.unsqueeze(0))
+            elif key in w_dram:
+                nc.sync.dma_start(
+                    out=raw[key][:].rearrange("r (a h) -> r a h", a=PACK),
+                    in_=w_dram[key].rearrange("(a r) h -> r a h", r=P),
+                )
+            else:
+                nc.sync.dma_start(
+                    out=raw[key][:],
+                    in_=xf[BLK * key : BLK * (key + 1), :].rearrange("(p j) h -> p (j h)", j=PACK),
+                )
+
+        g1s = {}
+        tps = {}
+
+        def th(key, b, tag):
+            if key not in g1s:
+                g1s[key] = work.tile([P, PACK * H], BF16, name="g1", tag="g1", bufs=3, align_bytes=64)
+            srcw = raw[key][:].bitcast(F32)
+            nbufs = TP_BUFS if tag == "tp" else 1
+            tp = psum.tile([P, 4, P], F32, name="tp", tag=tag, bufs=nbufs)
+            tps[(key, b)] = tp
+            for jj in range(2):
+                for u in range(2):
+                    col = 256 * (2 * b + jj) + 128 * u
+                    nc.tensor.transpose(tp[:, 2 * jj + u, :], srcw[:, col : col + P], ident[:])
+
+        def eh(key, b, engine):
+            gw = g1s[key][:].bitcast(F32).rearrange("p (j r u) -> p j r u", j=PACK, u=2)
+            src_view = tps[(key, b)][:].rearrange("p (jj u) r -> p jj r u", u=2)
+            if engine == "v":
+                nc.vector.tensor_copy(out=gw[:, 2 * b : 2 * b + 2, :, :], in_=src_view)
+            else:
+                nc.scalar.copy(out=gw[:, 2 * b : 2 * b + 2, :, :], in_=src_view)
+
+        def quant(grouped, codes, scales):
+            nc.vector.quantize_mx(out=codes[:].bitcast(FP8X4), scales=scales[:], in_=grouped)
+
+        xq = {}
+
+        def q1(key):
+            if key in w_dram:
+                q = const.tile([P, H], U32, name="wq_" + key, align_bytes=64)
+                s = const.tile([P, H], U8, name="ws_" + key, align_bytes=64)
+            else:
+                q = work.tile([P, H], U32, name="xq", tag="xq", bufs=3, align_bytes=64)
+                s = work.tile([P, H], U8, name="xs", tag="xs", bufs=3, align_bytes=64)
+            quant(g1s[key][:], q, s)
+            xq[key] = (q, s)
+
+        def regroup(dst, src, lo, hi, engine):
+            if engine == "g":
+                nc.gpsimd.tensor_scalar(
+                    out=dst[:, lo:hi, :], in0=src[:, :, lo:hi].rearrange("p t h -> p h t"),
+                    scalar1=1.0, scalar2=0.0, op0=ALU.mult, op1=ALU.add,
+                )
+                return
+            d = dst[:, lo:hi, :].rearrange("p (c i) t -> p c t i", i=4)
+            s = src[:, :, lo:hi].rearrange("p t (c i) -> p c t i", i=4)
+            if engine == "v":
+                nc.vector.tensor_copy(out=d, in_=s)
+            else:
+                nc.scalar.copy(out=d, in_=s)
+
+        xm = {}
+        g3s = {}
+
+        def r3(c, engine, lo, hi):
+            if c not in g3s:
+                g3s[c] = work.tile([P, H, PACK], BF16, name="g3", tag="g3", bufs=3, align_bytes=64)
+            regroup(g3s[c], raw[c][:].rearrange("p (t h) -> p t h", t=PACK), lo, hi, engine)
+
+        def q3(c):
+            q = xpool.tile([P, H], U32, name="xmq%d" % c, align_bytes=64)
+            s = xpool.tile([P, H], U8, name="xms%d" % c, align_bytes=64)
+            quant(g3s[c][:].rearrange("p h t -> p (h t)"), q, s)
+            xm[c] = (q, s)
+
+        cs = {}
+        pss = {}
+        bias_bc = const.tile([P, H], F32, name="bias_bc")
+
+        def bias():
+            bias_ps = psum.tile([P, H], F32, name="bias_ps", tag="ps", bufs=PS_BUFS)
+            nc.tensor.matmul(out=bias_ps[:], lhsT=ones_b[:], rhs=zb[:, 0:H], start=True, stop=True)
+            nc.scalar.copy(out=bias_bc[:], in_=bias_ps[:])
+
+        def s1mm(c, j):
+            ps = psum.tile([P, H], F32, name="ps", tag="ps", bufs=PS_BUFS)
+            pss[(c, j)] = ps
+            q, s = xq[c]
+            cols = slice(P * j, P * (j + 1))
+            for n, key in enumerate(("f", "p")):
+                wq, ws = xq[key]
+                nc.tensor.matmul_mx(
+                    out=ps[:],
+                    lhsT=q[:, cols].bitcast(FP8X4),
+                    lhsT_scale=s[:, cols],
+                    rhs=wq[:].bitcast(FP8X4),
+                    rhs_scale=ws[:],
+                    start=(n == 0),
+                    stop=(n == 1),
+                )
+
+        def badd(c, j):
+            if j == 0:
+                cs[c] = work.tile([P, PACK, H], F32, name="cs", tag="cs", bufs=3)
+            nc.vector.tensor_tensor(out=cs[c][:, j, :], in0=pss[(c, j)][:], in1=bias_bc[:], op=ALU.add)
+
+        def store(c):
+            nc.sync.dma_start(
+                out=of[BLK * c : BLK * (c + 1), :].rearrange("(p j) o -> p (j o)", j=PACK),
+                in_=cs[c][:].rearrange("p j o -> p (j o)"),
+            )
+
+        g2s = {}
+
+        def r2(c, engine, lo, hi):
+            if c not in g2s:
+                g2s[c] = work.tile([P, H, PACK], BF16, name="g2", tag="g2", bufs=2, align_bytes=64)
+            regroup(g2s[c], cs[c], lo, hi, engine)
+
+        cq = {}
+
+        def q2(c):
+            q = work.tile([P, H], U32, name="cq", tag="cq", bufs=4, align_bytes=64)
+            s = work.tile([P, H], U8, name="cqs", tag="cqs", bufs=4, align_bytes=64)
+            quant(g2s[c][:].rearrange("p h t -> p (h t)"), q, s)
+            cq[c] = (q, s)
+
+        hebb = {}
+
+        def s2(c, ts):
+            q, s = xm[c]
+            rq, rs = cq[c]
+            for t in ts:
+                if c == 0:
+                    hebb[t] = psum.tile([P, H], F32, name="hebb%d" % t, tag="hb%d" % t)
+                cols = slice(P * t, P * (t + 1))
+                nc.tensor.matmul_mx(
+                    out=hebb[t][:],
+                    lhsT=q[:, cols].bitcast(FP8X4),
+                    lhsT_scale=s[:, cols],
+                    rhs=rq[:].bitcast(FP8X4),
+                    rhs_scale=rs[:],
+                    start=(c == 0),
+                    stop=(c == NB - 1),
+                )
+
+        gain_t = const.tile([P, 1], F32, name="gain_t")
+
+        def gain():
+            rs_ps = psum.tile([P, 32], F32, name="rs_ps", tag="tp", bufs=TP_BUFS)
+            nc.tensor.matmul(out=rs_ps[:], lhsT=ones_b[:], rhs=zb[:, 512:544], start=True, stop=True)
+            rs_sb = const.tile([P, 32], F32, name="rs_sb")
+            nc.scalar.copy(out=rs_sb[:], in_=rs_ps[:])
+            nc.vector.scalar_tensor_tensor(
+                out=gain_t[:], in0=rs_sb[:, 0:1], scalar=1.0 / ROWS, in1=rs_sb[:, 16:17],
+                op0=ALU.mult, op1=ALU.mult,
+            )
+
+        def fin():
+            nw = const.tile([P, PACK, H], F32, name="nw")
+            junk = const.tile([P, H], F32, name="junk")
+            acc = const.tile([P, PACK], F32, name="acc")
+            tot = psum.tile([P, 1], F32, name="tot", tag="ps", bufs=PS_BUFS)
+            for t in range(PACK):
+                nc.vector.scalar_tensor_tensor(
+                    out=nw[:, t, :], in0=hebb[t][:], scalar=gain_t[:, 0:1],
+                    in1=raw["p"][:, H * t : H * (t + 1)], op0=ALU.mult, op1=ALU.add,
+                )
+                nc.scalar.activation(out=junk[:], in_=nw[:, t, :], func=ACT.Square, accum_out=acc[:, t : t + 1])
+                nc.tensor.matmul(out=tot[:], lhsT=ones_f[:], rhs=acc[:, t : t + 1], start=(t == 0), stop=(t == PACK - 1))
+            rinv = const.tile([P, 1], F32, name="rinv")
+            rraw = const.tile([P, 1], F32, name="rraw")
+            nc.scalar.activation(out=rraw[:], in_=tot[:], func=ACT.Abs_reciprocal_sqrt)
+            nc.vector.tensor_scalar_min(out=rinv[:], in0=rraw[:], scalar1=1.0)
+            res = const.tile([P, PACK, H], F32, name="res")
+            o1 = out_1.rearrange("(t p) j -> p t j", p=P)
+            for t in range(PACK):
+                nc.vector.tensor_scalar_mul(out=res[:, t, :], in0=nw[:, t, :], scalar1=rinv[:, 0:1])
+                nc.sync.dma_start(out=o1[:, t, :], in_=res[:, t, :])
+
+        load(0)
+        load("f")
+        load("b")
+        load("p")
+        load(1)
+        load(2)
+        load(3)
+        load(4)
+        load(5)
+        load(6)
+        load(7)
+        load(8)
+        load(9)
+        load(10)
+        load(11)
+        load("r")
+        r3(0, "v", 0, 288)
+        th(0, 0, "hb2")
+        th(0, 1, "hb3")
+        eh(0, 0, "s")
+        eh(0, 1, "v")
+        r3(0, "s", 288, 512)
+        q1(0)
+        th("f", 0, "hb0")
+        th("f", 1, "hb1")
+        eh("f", 0, "s")
+        eh("f", 1, "v")
+        q1("f")
+        bias()
+        th("p", 0, "tp")
+        th("p", 1, "tp")
+        eh("p", 0, "s")
+        eh("p", 1, "v")
+        q1("p")
+        th(1, 0, "hb2")
+        th(1, 1, "hb3")
+        eh(1, 0, "s")
+        eh(1, 1, "v")
+        th(2, 0, "hb0")
+        th(2, 1, "hb1")
+        eh(2, 0, "s")
+        eh(2, 1, "s")
+        s1mm(0, 0)
+        s1mm(0, 1)
+        q3(0)
+        r3(1, "v", 0, 288)
+        r3(1, "s", 288, 512)
+        q1(1)
+        badd(0, 0)
+        s1mm(0, 2)
+        badd(0, 1)
+        s1mm(0, 3)
+        r3(2, "v", 0, 224)
+        badd(0, 2)
+        s1mm(1, 0)
+        badd(0, 3)
+        s1mm(1, 1)
+        store(0)
+        r2(0, "s", 0, 512)
+        q1(2)
+        th(3, 0, "tp")
+        th(3, 1, "tp")
+        eh(3, 0, "s")
+        eh(3, 1, "s")
+        r3(2, "s", 224, 512)
+        badd(1, 0)
+        s1mm(1, 2)
+        badd(1, 1)
+        s1mm(1, 3)
+        q3(1)
+        r3(3, "v", 0, 224)
+        badd(1, 2)
+        s1mm(2, 0)
+        badd(1, 3)
+        s1mm(2, 1)
+        store(1)
+        r2(1, "s", 0, 512)
+        q2(0)
+        q1(3)
+        th(4, 0, "tp")
+        th(4, 1, "tp")
+        eh(4, 0, "s")
+        eh(4, 1, "s")
+        r3(3, "s", 224, 512)
+        badd(2, 0)
+        s1mm(2, 2)
+        badd(2, 1)
+        s1mm(2, 3)
+        q3(2)
+        r3(4, "v", 0, 224)
+        s2(0, (0, 1, 2, 3,))
+        badd(2, 2)
+        s1mm(3, 0)
+        badd(2, 3)
+        s1mm(3, 1)
+        store(2)
+        r2(2, "s", 0, 512)
+        q2(1)
+        q1(4)
+        th(5, 0, "tp")
+        th(5, 1, "tp")
+        eh(5, 0, "s")
+        eh(5, 1, "s")
+        r3(4, "s", 224, 512)
+        badd(3, 0)
+        s1mm(3, 2)
+        badd(3, 1)
+        s1mm(3, 3)
+        q3(3)
+        r3(5, "v", 0, 224)
+        s2(1, (0, 1, 2, 3,))
+        badd(3, 2)
+        s1mm(4, 0)
+        badd(3, 3)
+        s1mm(4, 1)
+        store(3)
+        r2(3, "s", 0, 512)
+        q2(2)
+        q1(5)
+        th(6, 0, "tp")
+        th(6, 1, "tp")
+        eh(6, 0, "s")
+        eh(6, 1, "s")
+        r3(5, "s", 224, 512)
+        badd(4, 0)
+        s1mm(4, 2)
+        badd(4, 1)
+        s1mm(4, 3)
+        q3(4)
+        r3(6, "v", 0, 224)
+        s2(2, (0, 1, 2, 3,))
+        badd(4, 2)
+        s1mm(5, 0)
+        badd(4, 3)
+        s1mm(5, 1)
+        store(4)
+        r2(4, "s", 0, 512)
+        q2(3)
+        q1(6)
+        th(7, 0, "tp")
+        th(7, 1, "tp")
+        eh(7, 0, "s")
+        eh(7, 1, "s")
+        r3(6, "s", 224, 512)
+        badd(5, 0)
+        s1mm(5, 2)
+        badd(5, 1)
+        s1mm(5, 3)
+        q3(5)
+        r3(7, "v", 0, 224)
+        s2(3, (0, 1, 2, 3,))
+        badd(5, 2)
+        s1mm(6, 0)
+        badd(5, 3)
+        s1mm(6, 1)
+        store(5)
+        r2(5, "s", 0, 512)
+        q2(4)
+        q1(7)
+        th(8, 0, "tp")
+        th(8, 1, "tp")
+        eh(8, 0, "s")
+        eh(8, 1, "s")
+        r3(7, "s", 224, 512)
+        gain()
+        badd(6, 0)
+        s1mm(6, 2)
+        badd(6, 1)
+        s1mm(6, 3)
+        q3(6)
+        r3(8, "v", 0, 224)
+        s2(4, (0, 1, 2, 3,))
+        badd(6, 2)
+        s1mm(7, 0)
+        badd(6, 3)
+        s1mm(7, 1)
+        store(6)
+        r2(6, "s", 0, 512)
+        q2(5)
+        q1(8)
+        th(9, 0, "tp")
+        th(9, 1, "tp")
+        eh(9, 0, "s")
+        eh(9, 1, "s")
+        r3(8, "s", 224, 512)
+        badd(7, 0)
+        s1mm(7, 2)
+        badd(7, 1)
+        s1mm(7, 3)
+        q3(7)
+        r3(9, "v", 0, 224)
+        s2(5, (0, 1, 2, 3,))
+        badd(7, 2)
+        s1mm(8, 0)
+        badd(7, 3)
+        s1mm(8, 1)
+        store(7)
+        r2(7, "s", 0, 512)
+        q2(6)
+        q1(9)
+        th(10, 0, "tp")
+        th(10, 1, "tp")
+        eh(10, 0, "s")
+        eh(10, 1, "s")
+        r3(9, "s", 224, 512)
+        badd(8, 0)
+        s1mm(8, 2)
+        badd(8, 1)
+        s1mm(8, 3)
+        q3(8)
+        r3(10, "v", 0, 224)
+        s2(6, (0, 1, 2, 3,))
+        badd(8, 2)
+        s1mm(9, 0)
+        badd(8, 3)
+        s1mm(9, 1)
+        store(8)
+        r2(8, "s", 0, 512)
+        q2(7)
+        q1(10)
+        th(11, 0, "tp")
+        th(11, 1, "tp")
+        eh(11, 0, "s")
+        eh(11, 1, "s")
+        r3(10, "s", 224, 512)
+        badd(9, 0)
+        s1mm(9, 2)
+        badd(9, 1)
+        s1mm(9, 3)
+        q3(9)
+        r3(11, "v", 0, 224)
+        s2(7, (0, 1, 2, 3,))
+        badd(9, 2)
+        s1mm(10, 0)
+        badd(9, 3)
+        s1mm(10, 1)
+        store(9)
+        r2(9, "s", 0, 512)
+        q2(8)
+        q1(11)
+        r3(11, "s", 224, 512)
+        badd(10, 0)
+        s1mm(10, 2)
+        badd(10, 1)
+        s1mm(10, 3)
+        q3(10)
+        s2(8, (0, 1, 2, 3,))
+        badd(10, 2)
+        s1mm(11, 0)
+        badd(10, 3)
+        s1mm(11, 1)
+        store(10)
+        r2(10, "s", 0, 512)
+        q2(9)
+        badd(11, 0)
+        s1mm(11, 2)
+        badd(11, 1)
+        s1mm(11, 3)
+        q3(11)
+        q2(10)
+        s2(9, (0, 1, 2, 3,))
+        badd(11, 2)
+        badd(11, 3)
+        store(11)
+        r2(11, "v", 0, 320)
+        r2(11, "s", 320, 512)
+        s2(10, (0, 1, 2, 3,))
+        q2(11)
+        s2(11, (0, 1, 2, 3,))
+        fin()

@@ -20,6 +20,10 @@ NB = ROWS // BLK
 FLOPS = 3 * 2 * ROWS * H * H
 PS_BUFS = 2
 TP_BUFS = 2
+G2 = 160
+G3 = 160
+H1S = 256
+TV = 192
 
 
 def tile_neuroplasticitylayer_t_kernel(
@@ -129,7 +133,7 @@ def tile_neuroplasticitylayer_t_kernel(
 
         def r3(c, engine, lo, hi):
             if c not in g3s:
-                g3s[c] = work.tile([P, H, PACK], BF16, name="g3", tag="g3", bufs=3, align_bytes=64)
+                g3s[c] = work.tile([P, H, PACK], BF16, name="g3", tag="g3", bufs=2, align_bytes=64)
             regroup(g3s[c], raw[c][:].rearrange("p (t h) -> p t h", t=PACK), lo, hi, engine)
 
         def q3(c):
@@ -239,277 +243,84 @@ def tile_neuroplasticitylayer_t_kernel(
             nc.vector.tensor_scalar_min(out=rinv[:], in0=rraw[:], scalar1=1.0)
             res = const.tile([P, PACK, H], F32, name="res")
             o1 = out_1.rearrange("(t p) j -> p t j", p=P)
-            for t in range(PACK):
-                nc.vector.tensor_scalar_mul(out=res[:, t, :], in0=nw[:, t, :], scalar1=rinv[:, 0:1])
+            nc.scalar.activation(out=res[:, 0, :], in_=nw[:, 0, :], func=ACT.Copy, scale=rinv[:, 0:1])
+            for t in (1, 2, 0, 3):
+                if t > 0:
+                    nc.vector.tensor_scalar_mul(out=res[:, t, :], in0=nw[:, t, :], scalar1=rinv[:, 0:1])
                 nc.sync.dma_start(out=o1[:, t, :], in_=res[:, t, :])
 
-        load(0)
-        load("f")
-        load("b")
-        load("p")
-        load(1)
-        load(2)
-        load(3)
-        load(4)
-        load(5)
-        load(6)
-        load(7)
-        load(8)
-        load(9)
-        load(10)
-        load(11)
-        load("r")
-        r3(0, "v", 0, 288)
+        for key in [0, "f", "b", "p"] + list(range(1, NB)) + ["r"]:
+            load(key)
+        r3(0, "v", 0, 512)
         th(0, 0, "hb2")
         th(0, 1, "hb3")
         eh(0, 0, "s")
-        eh(0, 1, "v")
-        r3(0, "s", 288, 512)
-        q1(0)
+        eh(0, 1, "s")
         th("f", 0, "hb0")
         th("f", 1, "hb1")
+        q1(0)
         eh("f", 0, "s")
         eh("f", 1, "v")
-        q1("f")
         bias()
         th("p", 0, "tp")
         th("p", 1, "tp")
+        q1("f")
         eh("p", 0, "s")
         eh("p", 1, "v")
         q1("p")
         th(1, 0, "hb2")
         th(1, 1, "hb3")
-        eh(1, 0, "s")
-        eh(1, 1, "v")
-        th(2, 0, "hb0")
-        th(2, 1, "hb1")
-        eh(2, 0, "s")
-        eh(2, 1, "s")
         s1mm(0, 0)
         s1mm(0, 1)
         q3(0)
-        r3(1, "v", 0, 288)
-        r3(1, "s", 288, 512)
+        eh(1, 0, "s")
+        eh(1, 1, "s")
+        th(2, 0, "tp")
+        th(2, 1, "tp")
+        r3(1, "s", 0, H1S)
+        r3(1, "v", H1S, 512)
         q1(1)
-        badd(0, 0)
-        s1mm(0, 2)
-        badd(0, 1)
-        s1mm(0, 3)
-        r3(2, "v", 0, 224)
-        badd(0, 2)
-        s1mm(1, 0)
-        badd(0, 3)
-        s1mm(1, 1)
-        store(0)
-        r2(0, "s", 0, 512)
-        q1(2)
-        th(3, 0, "tp")
-        th(3, 1, "tp")
-        eh(3, 0, "s")
-        eh(3, 1, "s")
-        r3(2, "s", 224, 512)
-        badd(1, 0)
-        s1mm(1, 2)
-        badd(1, 1)
-        s1mm(1, 3)
-        q3(1)
-        r3(3, "v", 0, 224)
-        badd(1, 2)
-        s1mm(2, 0)
-        badd(1, 3)
-        s1mm(2, 1)
-        store(1)
-        r2(1, "s", 0, 512)
-        q2(0)
-        q1(3)
-        th(4, 0, "tp")
-        th(4, 1, "tp")
-        eh(4, 0, "s")
-        eh(4, 1, "s")
-        r3(3, "s", 224, 512)
-        badd(2, 0)
-        s1mm(2, 2)
-        badd(2, 1)
-        s1mm(2, 3)
-        q3(2)
-        r3(4, "v", 0, 224)
-        s2(0, (0, 1, 2, 3,))
-        badd(2, 2)
-        s1mm(3, 0)
-        badd(2, 3)
-        s1mm(3, 1)
-        store(2)
-        r2(2, "s", 0, 512)
-        q2(1)
-        q1(4)
-        th(5, 0, "tp")
-        th(5, 1, "tp")
-        eh(5, 0, "s")
-        eh(5, 1, "s")
-        r3(4, "s", 224, 512)
-        badd(3, 0)
-        s1mm(3, 2)
-        badd(3, 1)
-        s1mm(3, 3)
-        q3(3)
-        r3(5, "v", 0, 224)
-        s2(1, (0, 1, 2, 3,))
-        badd(3, 2)
-        s1mm(4, 0)
-        badd(3, 3)
-        s1mm(4, 1)
-        store(3)
-        r2(3, "s", 0, 512)
-        q2(2)
-        q1(5)
-        th(6, 0, "tp")
-        th(6, 1, "tp")
-        eh(6, 0, "s")
-        eh(6, 1, "s")
-        r3(5, "s", 224, 512)
-        badd(4, 0)
-        s1mm(4, 2)
-        badd(4, 1)
-        s1mm(4, 3)
-        q3(4)
-        r3(6, "v", 0, 224)
-        s2(2, (0, 1, 2, 3,))
-        badd(4, 2)
-        s1mm(5, 0)
-        badd(4, 3)
-        s1mm(5, 1)
-        store(4)
-        r2(4, "s", 0, 512)
-        q2(3)
-        q1(6)
-        th(7, 0, "tp")
-        th(7, 1, "tp")
-        eh(7, 0, "s")
-        eh(7, 1, "s")
-        r3(6, "s", 224, 512)
-        badd(5, 0)
-        s1mm(5, 2)
-        badd(5, 1)
-        s1mm(5, 3)
-        q3(5)
-        r3(7, "v", 0, 224)
-        s2(3, (0, 1, 2, 3,))
-        badd(5, 2)
-        s1mm(6, 0)
-        badd(5, 3)
-        s1mm(6, 1)
-        store(5)
-        r2(5, "s", 0, 512)
-        q2(4)
-        q1(7)
-        th(8, 0, "tp")
-        th(8, 1, "tp")
-        eh(8, 0, "s")
-        eh(8, 1, "s")
-        r3(7, "s", 224, 512)
-        gain()
-        badd(6, 0)
-        s1mm(6, 2)
-        badd(6, 1)
-        s1mm(6, 3)
-        q3(6)
-        r3(8, "v", 0, 224)
-        s2(4, (0, 1, 2, 3,))
-        badd(6, 2)
-        s1mm(7, 0)
-        badd(6, 3)
-        s1mm(7, 1)
-        store(6)
-        r2(6, "s", 0, 512)
-        q2(5)
-        q1(8)
-        th(9, 0, "tp")
-        th(9, 1, "tp")
-        eh(9, 0, "s")
-        eh(9, 1, "s")
-        r3(8, "s", 224, 512)
-        badd(7, 0)
-        s1mm(7, 2)
-        badd(7, 1)
-        s1mm(7, 3)
-        q3(7)
-        r3(9, "v", 0, 224)
-        s2(5, (0, 1, 2, 3,))
-        badd(7, 2)
-        s1mm(8, 0)
-        badd(7, 3)
-        s1mm(8, 1)
-        store(7)
-        r2(7, "s", 0, 512)
-        q2(6)
-        q1(9)
-        th(10, 0, "tp")
-        th(10, 1, "tp")
-        eh(10, 0, "s")
-        eh(10, 1, "s")
-        r3(9, "s", 224, 512)
-        badd(8, 0)
-        s1mm(8, 2)
-        badd(8, 1)
-        s1mm(8, 3)
-        q3(8)
-        r3(10, "v", 0, 224)
-        s2(6, (0, 1, 2, 3,))
-        badd(8, 2)
-        s1mm(9, 0)
-        badd(8, 3)
-        s1mm(9, 1)
-        store(8)
-        r2(8, "s", 0, 512)
-        q2(7)
-        q1(10)
-        th(11, 0, "tp")
-        th(11, 1, "tp")
-        eh(11, 0, "s")
-        eh(11, 1, "s")
-        r3(10, "s", 224, 512)
-        badd(9, 0)
-        s1mm(9, 2)
-        badd(9, 1)
-        s1mm(9, 3)
-        q3(9)
-        r3(11, "v", 0, 224)
-        s2(7, (0, 1, 2, 3,))
-        badd(9, 2)
-        s1mm(10, 0)
-        badd(9, 3)
-        s1mm(10, 1)
-        store(9)
-        r2(9, "s", 0, 512)
-        q2(8)
-        q1(11)
-        r3(11, "s", 224, 512)
-        badd(10, 0)
-        s1mm(10, 2)
-        badd(10, 1)
-        s1mm(10, 3)
-        q3(10)
-        s2(8, (0, 1, 2, 3,))
-        badd(10, 2)
-        s1mm(11, 0)
-        badd(10, 3)
-        s1mm(11, 1)
-        store(10)
-        r2(10, "s", 0, 512)
-        q2(9)
-        badd(11, 0)
-        s1mm(11, 2)
-        badd(11, 1)
-        s1mm(11, 3)
-        q3(11)
-        q2(10)
-        s2(9, (0, 1, 2, 3,))
-        badd(11, 2)
-        badd(11, 3)
-        store(11)
-        r2(11, "v", 0, 320)
-        r2(11, "s", 320, 512)
-        s2(10, (0, 1, 2, 3,))
-        q2(11)
-        s2(11, (0, 1, 2, 3,))
+        r3(2, "g", 0, G3)
+        r3(2, "s", G3, 512)
+        for i in range(NB + 1):
+            if i + 2 < NB:
+                eh(i + 2, 0, "s")
+                eh(i + 2, 1, "s")
+            if i < NB:
+                badd(i, 0)
+                badd(i, 1)
+                s1mm(i, 2)
+                s1mm(i, 3)
+            if i + 1 < NB:
+                q3(i + 1)
+            if i + 3 < NB:
+                r3(i + 3, "g", 0, G3)
+                r3(i + 3, "s", G3, 512)
+            if 1 <= i and i + 2 < NB:
+                q2(i - 1)
+            if 2 <= i:
+                s2(i - 2, (0, 1, 2, 3))
+            if i < NB:
+                badd(i, 2)
+                badd(i, 3)
+                store(i)
+            if i < NB - 1:
+                r2(i, "g", 0, G2)
+                r2(i, "s", G2, 512)
+            if i == NB - 1:
+                r2(i, "v", 0, TV)
+                r2(i, "s", TV, 512)
+            if i + 1 < NB:
+                s1mm(i + 1, 0)
+                s1mm(i + 1, 1)
+            if i + 2 < NB:
+                q1(i + 2)
+            elif i >= 1:
+                q2(i - 1)
+            if i == NB // 2:
+                gain()
+            if i + 3 < NB:
+                th(i + 3, 0, "tp")
+                th(i + 3, 1, "tp")
+        s2(NB - 1, (0, 1, 2, 3))
         fin()

@@ -23,7 +23,7 @@ TP_BUFS = 2
 G2 = 160
 G3 = 160
 H1S = 256
-TV = 192
+TV = 256
 
 
 def tile_neuroplasticitylayer_t_kernel(
@@ -215,11 +215,14 @@ def tile_neuroplasticitylayer_t_kernel(
 
         gain_t = const.tile([P, 1], F32, name="gain_t")
 
-        def gain():
+        rs_sb = const.tile([P, 32], F32, name="rs_sb")
+
+        def gain_a():
             rs_ps = psum.tile([P, 32], F32, name="rs_ps", tag="tp", bufs=TP_BUFS)
             nc.tensor.matmul(out=rs_ps[:], lhsT=ones_b[:], rhs=zb[:, 512:544], start=True, stop=True)
-            rs_sb = const.tile([P, 32], F32, name="rs_sb")
             nc.scalar.copy(out=rs_sb[:], in_=rs_ps[:])
+
+        def gain_b():
             nc.vector.scalar_tensor_tensor(
                 out=gain_t[:], in0=rs_sb[:, 0:1], scalar=1.0 / ROWS, in1=rs_sb[:, 16:17],
                 op0=ALU.mult, op1=ALU.mult,
@@ -282,45 +285,44 @@ def tile_neuroplasticitylayer_t_kernel(
         q1(1)
         r3(2, "g", 0, G3)
         r3(2, "s", G3, 512)
-        for i in range(NB + 1):
+        for i in range(NB):
             if i + 2 < NB:
                 eh(i + 2, 0, "s")
                 eh(i + 2, 1, "s")
-            if i < NB:
-                badd(i, 0)
-                badd(i, 1)
-                s1mm(i, 2)
-                s1mm(i, 3)
-            if i + 1 < NB:
+            badd(i, 0)
+            badd(i, 1)
+            s1mm(i, 2)
+            s1mm(i, 3)
+            if i + 1 < NB - 1:
                 q3(i + 1)
             if i + 3 < NB:
                 r3(i + 3, "g", 0, G3)
                 r3(i + 3, "s", G3, 512)
-            if 1 <= i and i + 2 < NB:
+            if i >= 1:
                 q2(i - 1)
-            if 2 <= i:
+            if i >= 2:
                 s2(i - 2, (0, 1, 2, 3))
-            if i < NB:
-                badd(i, 2)
-                badd(i, 3)
-                store(i)
+            badd(i, 2)
+            badd(i, 3)
+            store(i)
             if i < NB - 1:
                 r2(i, "g", 0, G2)
                 r2(i, "s", G2, 512)
-            if i == NB - 1:
-                r2(i, "v", 0, TV)
-                r2(i, "s", TV, 512)
-            if i + 1 < NB:
                 s1mm(i + 1, 0)
                 s1mm(i + 1, 1)
+            else:
+                r2(i, "v", 0, TV)
+                r2(i, "s", TV, 512)
+                gain_a()
             if i + 2 < NB:
                 q1(i + 2)
-            elif i >= 1:
-                q2(i - 1)
-            if i == NB // 2:
-                gain()
+            elif i == NB - 2:
+                q3(NB - 1)
             if i + 3 < NB:
                 th(i + 3, 0, "tp")
                 th(i + 3, 1, "tp")
+        s2(NB - 2, (0, 1, 2, 3))
+        q2(NB - 1)
+        gain_b()
         s2(NB - 1, (0, 1, 2, 3))
         fin()

@@ -20,10 +20,10 @@ NB = ROWS // BLK
 FLOPS = 3 * 2 * ROWS * H * H
 PS_BUFS = 2
 TP_BUFS = 2
-G2 = 160
+G2 = 176
 G3 = 160
-H1S = 256
-TV = 256
+H1S = 192
+TV = 288
 
 
 def tile_neuroplasticitylayer_t_kernel(
@@ -59,7 +59,8 @@ def tile_neuroplasticitylayer_t_kernel(
             raw[c] = xpool.tile([P, PACK * H], BF16, name="x_sb%d" % c)
         w_dram = {"f": fixed_w, "p": plastic_weights}
 
-        def load(key):
+        def load(key, half=None):
+            a0, a1 = (0, PACK) if half is None else (2 * half, 2 * half + 2)
             if key == "b":
                 nc.sync.dma_start(out=zb[0:1, 0:H], in_=fixed_b.unsqueeze(0))
             elif key == "r":
@@ -67,13 +68,13 @@ def tile_neuroplasticitylayer_t_kernel(
                 nc.sync.dma_start(out=zb[0:1, 528:529], in_=hebbian_strength.unsqueeze(0))
             elif key in w_dram:
                 nc.sync.dma_start(
-                    out=raw[key][:].rearrange("r (a h) -> r a h", a=PACK),
-                    in_=w_dram[key].rearrange("(a r) h -> r a h", r=P),
+                    out=raw[key][:, H * a0 : H * a1].rearrange("r (a h) -> r a h", h=H),
+                    in_=w_dram[key].rearrange("(a r) h -> r a h", r=P)[:, a0:a1, :],
                 )
             else:
                 nc.sync.dma_start(
-                    out=raw[key][:],
-                    in_=xf[BLK * key : BLK * (key + 1), :].rearrange("(p j) h -> p (j h)", j=PACK),
+                    out=raw[key][:, H * a0 : H * a1].rearrange("p (j h) -> p j h", h=H),
+                    in_=xf[BLK * key : BLK * (key + 1), :].rearrange("(p j) h -> p j h", j=PACK)[:, a0:a1, :],
                 )
 
         g1s = {}
@@ -252,7 +253,12 @@ def tile_neuroplasticitylayer_t_kernel(
                     nc.vector.tensor_scalar_mul(out=res[:, t, :], in0=nw[:, t, :], scalar1=rinv[:, 0:1])
                 nc.sync.dma_start(out=o1[:, t, :], in_=res[:, t, :])
 
-        for key in [0, "f", "b", "p"] + list(range(1, NB)) + ["r"]:
+        for key in (0, "f", "p"):
+            load(key, 0)
+            load(key, 1)
+            if key == "f":
+                load("b")
+        for key in list(range(1, NB)) + ["r"]:
             load(key)
         r3(0, "v", 0, 512)
         th(0, 0, "hb2")

@@ -22,7 +22,6 @@ PS_BUFS = 2
 TP_BUFS = 2
 G2 = 176
 G3 = 160
-H1S = 192
 TV = 288
 
 
@@ -143,6 +142,7 @@ def tile_neuroplasticitylayer_t_kernel(
             quant(g3s[c][:].rearrange("p h t -> p (h t)"), q, s)
             xm[c] = (q, s)
 
+        hold = const.tile([P, 1], BF16, name="hold")
         cs = {}
         pss = {}
         bias_bc = const.tile([P, H], F32, name="bias_bc")
@@ -264,31 +264,33 @@ def tile_neuroplasticitylayer_t_kernel(
         th(0, 0, "hb2")
         th(0, 1, "hb3")
         eh(0, 0, "s")
-        eh(0, 1, "s")
+        eh(0, 1, "v")
         th("f", 0, "hb0")
         th("f", 1, "hb1")
+        q3(0)
         q1(0)
         eh("f", 0, "s")
-        eh("f", 1, "v")
-        bias()
+        eh("f", 1, "s")
         th("p", 0, "tp")
         th("p", 1, "tp")
         q1("f")
         eh("p", 0, "s")
-        eh("p", 1, "v")
+        eh("p", 1, "s")
+        bias()
+        r3(1, "v", 0, 384)
         q1("p")
         th(1, 0, "hb2")
         th(1, 1, "hb3")
         s1mm(0, 0)
         s1mm(0, 1)
-        q3(0)
+        r3(1, "v", 384, 512)
         eh(1, 0, "s")
         eh(1, 1, "s")
         th(2, 0, "tp")
         th(2, 1, "tp")
-        r3(1, "s", 0, H1S)
-        r3(1, "v", H1S, 512)
-        q1(1)
+        nc.gpsimd.tensor_scalar(
+            out=hold[:], in0=g3s[1][:, 511, 3:4], scalar1=1.0, scalar2=0.0, op0=ALU.mult, op1=ALU.add
+        )
         r3(2, "g", 0, G3)
         r3(2, "s", G3, 512)
         for i in range(NB):
@@ -299,6 +301,8 @@ def tile_neuroplasticitylayer_t_kernel(
             badd(i, 1)
             s1mm(i, 2)
             s1mm(i, 3)
+            if i == 0:
+                q1(1)
             if i + 1 < NB - 1:
                 q3(i + 1)
             if i + 3 < NB:

@@ -13,16 +13,17 @@ ACT = mybir.ActivationFunctionType
 
 P = 128
 H = 512
+HH = H // 2
 ROWS = 6144
 PACK = 4
 BLK = P * PACK
 NB = ROWS // BLK
+NP = NB // 2
 FLOPS = 3 * 2 * ROWS * H * H
-PS_BUFS = 2
-TP_BUFS = 2
-G2 = 176
-G3 = 160
-TV = 288
+G2 = 184
+G3 = 184
+V1 = 128
+TV = 256
 
 
 def tile_neuroplasticitylayer_t_kernel(
@@ -54,8 +55,11 @@ def tile_neuroplasticitylayer_t_kernel(
         raw = {}
         raw["f"] = const.tile([P, PACK * H], BF16, name="wf_raw")
         raw["p"] = const.tile([P, PACK * H], BF16, name="wp_raw")
-        for c in range(NB):
-            raw[c] = xpool.tile([P, PACK * H], BF16, name="x_sb%d" % c)
+        xr = {}
+        for pr in range(NP):
+            xr[pr] = xpool.tile([P, 2, PACK * H], BF16, name="x_sb%d" % pr)
+            for half in range(2):
+                raw[2 * pr + half] = xr[pr][:, half, :]
         w_dram = {"f": fixed_w, "p": plastic_weights}
 
         def load(key, half=None):
@@ -79,12 +83,22 @@ def tile_neuroplasticitylayer_t_kernel(
         g1s = {}
         tps = {}
 
-        def th(key, b, tag):
-            if key not in g1s:
-                g1s[key] = work.tile([P, PACK * H], BF16, name="g1", tag="g1", bufs=3, align_bytes=64)
+        def slot(key):
+            if key in w_dram:
+                return "w", 0 if key == "f" else 1
+            return key // 2, key % 2
+
+        def bank(tag):
+            if tag is None:
+                return psum.tile([P, 4, P], F32, name="ps", tag="ps", bufs=4)
+            return psum.tile([P, 4, P], F32, name="tp", tag=tag)
+
+        def th(key, b, tag=None):
+            pr, half = slot(key)
+            if pr not in g1s:
+                g1s[pr] = work.tile([P, 2, PACK * H], BF16, name="g1", tag="g1", bufs=2, align_bytes=64)
             srcw = raw[key][:].bitcast(F32)
-            nbufs = TP_BUFS if tag == "tp" else 1
-            tp = psum.tile([P, 4, P], F32, name="tp", tag=tag, bufs=nbufs)
+            tp = bank(tag)
             tps[(key, b)] = tp
             for jj in range(2):
                 for u in range(2):
@@ -92,7 +106,8 @@ def tile_neuroplasticitylayer_t_kernel(
                     nc.tensor.transpose(tp[:, 2 * jj + u, :], srcw[:, col : col + P], ident[:])
 
         def eh(key, b, engine):
-            gw = g1s[key][:].bitcast(F32).rearrange("p (j r u) -> p j r u", j=PACK, u=2)
+            pr, half = slot(key)
+            gw = g1s[pr][:, half, :].bitcast(F32).rearrange("p (j r u) -> p j r u", j=PACK, u=2)
             src_view = tps[(key, b)][:].rearrange("p (jj u) r -> p jj r u", u=2)
             if engine == "v":
                 nc.vector.tensor_copy(out=gw[:, 2 * b : 2 * b + 2, :, :], in_=src_view)
@@ -100,126 +115,163 @@ def tile_neuroplasticitylayer_t_kernel(
                 nc.scalar.copy(out=gw[:, 2 * b : 2 * b + 2, :, :], in_=src_view)
 
         def quant(grouped, codes, scales):
-            nc.vector.quantize_mx(out=codes[:].bitcast(FP8X4), scales=scales[:], in_=grouped)
+            nc.vector.quantize_mx(out=codes.bitcast(FP8X4), scales=scales, in_=grouped)
 
         xq = {}
 
-        def q1(key):
-            if key in w_dram:
-                q = const.tile([P, H], U32, name="wq_" + key, align_bytes=64)
-                s = const.tile([P, H], U8, name="ws_" + key, align_bytes=64)
+        def q1(pr, half=None):
+            if pr not in xq:
+                if pr == "w":
+                    q = const.tile([P, 2 * H], U32, name="wq", align_bytes=64)
+                    s = const.tile([P, 2 * H], U8, name="ws", align_bytes=64)
+                else:
+                    q = work.tile([P, 2 * H], U32, name="xq", tag="xq", bufs=2, align_bytes=64)
+                    s = work.tile([P, 2 * H], U8, name="xs", tag="xs", bufs=2, align_bytes=64)
+                xq[pr] = (q, s)
+            q, s = xq[pr]
+            if half is None:
+                quant(g1s[pr][:].rearrange("p k n -> p (k n)"), q[:], s[:])
             else:
-                q = work.tile([P, H], U32, name="xq", tag="xq", bufs=3, align_bytes=64)
-                s = work.tile([P, H], U8, name="xs", tag="xs", bufs=3, align_bytes=64)
-            quant(g1s[key][:], q, s)
-            xq[key] = (q, s)
+                cols = slice(H * half, H * (half + 1))
+                quant(g1s[pr][:, half, :], q[:, cols], s[:, cols])
 
         def regroup(dst, src, lo, hi, engine):
-            if engine == "g":
-                nc.gpsimd.tensor_scalar(
-                    out=dst[:, lo:hi, :], in0=src[:, :, lo:hi].rearrange("p t h -> p h t"),
-                    scalar1=1.0, scalar2=0.0, op0=ALU.mult, op1=ALU.add,
-                )
-                return
             d = dst[:, lo:hi, :].rearrange("p (c i) t -> p c t i", i=4)
             s = src[:, :, lo:hi].rearrange("p t (c i) -> p c t i", i=4)
             if engine == "v":
                 nc.vector.tensor_copy(out=d, in_=s)
-            else:
+            elif engine == "s":
                 nc.scalar.copy(out=d, in_=s)
+            else:
+                nc.gpsimd.tensor_scalar(
+                    out=dst[:, lo:hi, :], in0=src[:, :, lo:hi].rearrange("p t h -> p h t"),
+                    scalar1=1.0, scalar2=0.0, op0=ALU.mult, op1=ALU.add,
+                )
 
         xm = {}
         g3s = {}
 
         def r3(c, engine, lo, hi):
-            if c not in g3s:
-                g3s[c] = work.tile([P, H, PACK], BF16, name="g3", tag="g3", bufs=2, align_bytes=64)
-            regroup(g3s[c], raw[c][:].rearrange("p (t h) -> p t h", t=PACK), lo, hi, engine)
+            pr = c // 2
+            if pr not in g3s:
+                g3s[pr] = work.tile([P, 2, H, PACK], BF16, name="g3", tag="g3", bufs=2, align_bytes=64)
+            regroup(g3s[pr][:, c % 2], raw[c][:].rearrange("p (t h) -> p t h", t=PACK), lo, hi, engine)
 
-        def q3(c):
-            q = xpool.tile([P, H], U32, name="xmq%d" % c, align_bytes=64)
-            s = xpool.tile([P, H], U8, name="xms%d" % c, align_bytes=64)
-            quant(g3s[c][:].rearrange("p h t -> p (h t)"), q, s)
-            xm[c] = (q, s)
+        def q3(pr, half=None):
+            if pr not in xm:
+                q = xpool.tile([P, 2 * H], U32, name="xmq%d" % pr, align_bytes=64)
+                s = xpool.tile([P, 2 * H], U8, name="xms%d" % pr, align_bytes=64)
+                xm[pr] = (q, s)
+            q, s = xm[pr]
+            if half is None:
+                quant(g3s[pr][:].rearrange("p k h t -> p (k h t)"), q[:], s[:])
+            else:
+                cols = slice(H * half, H * (half + 1))
+                quant(g3s[pr][:, half].rearrange("p h t -> p (h t)"), q[:, cols], s[:, cols])
 
-        hold = const.tile([P, 1], BF16, name="hold")
         cs = {}
         pss = {}
         bias_bc = const.tile([P, H], F32, name="bias_bc")
 
         def bias():
-            bias_ps = psum.tile([P, H], F32, name="bias_ps", tag="ps", bufs=PS_BUFS)
+            bias_ps = psum.tile([P, H], F32, name="bias_ps", tag="hb0")
             nc.tensor.matmul(out=bias_ps[:], lhsT=ones_b[:], rhs=zb[:, 0:H], start=True, stop=True)
             nc.scalar.copy(out=bias_bc[:], in_=bias_ps[:])
 
-        def s1mm(c, j):
-            ps = psum.tile([P, H], F32, name="ps", tag="ps", bufs=PS_BUFS)
-            pss[(c, j)] = ps
-            q, s = xq[c]
-            cols = slice(P * j, P * (j + 1))
-            for n, key in enumerate(("f", "p")):
-                wq, ws = xq[key]
+        def mm(pr, n):
+            ps = psum.tile([P, H], F32, name="ps", tag="ps", bufs=4)
+            pss[(pr, n)] = ps
+            q, s = xq[pr]
+            wq, ws = xq["w"]
+            cols = slice(P * n, P * (n + 1))
+            for m in range(2):
+                wc = slice(H * m, H * (m + 1))
                 nc.tensor.matmul_mx(
                     out=ps[:],
                     lhsT=q[:, cols].bitcast(FP8X4),
                     lhsT_scale=s[:, cols],
-                    rhs=wq[:].bitcast(FP8X4),
-                    rhs_scale=ws[:],
-                    start=(n == 0),
-                    stop=(n == 1),
+                    rhs=wq[:, wc].bitcast(FP8X4),
+                    rhs_scale=ws[:, wc],
+                    start=(m == 0),
+                    stop=(m == 1),
                 )
 
-        def badd(c, j):
-            if j == 0:
-                cs[c] = work.tile([P, PACK, H], F32, name="cs", tag="cs", bufs=3)
-            nc.vector.tensor_tensor(out=cs[c][:, j, :], in0=pss[(c, j)][:], in1=bias_bc[:], op=ALU.add)
+        def badd(pr, n):
+            if n == 0:
+                cs[pr] = work.tile([P, 2, PACK, H], F32, name="cs", tag="cs", bufs=2)
+            nc.vector.tensor_tensor(out=cs[pr][:, n // PACK, n % PACK, :], in0=pss[(pr, n)][:], in1=bias_bc[:], op=ALU.add)
+            if n % PACK == PACK - 1:
+                c = 2 * pr + n // PACK
+                nc.sync.dma_start(
+                    out=of[BLK * c : BLK * (c + 1), :].rearrange("(p j) o -> p (j o)", j=PACK),
+                    in_=cs[pr][:, n // PACK].rearrange("p j o -> p (j o)"),
+                )
 
-        def store(c):
-            nc.sync.dma_start(
-                out=of[BLK * c : BLK * (c + 1), :].rearrange("(p j) o -> p (j o)", j=PACK),
-                in_=cs[c][:].rearrange("p j o -> p (j o)"),
+        def regroup_pair(dst, src, cols):
+            nc.gpsimd.tensor_scalar(
+                out=dst[:, :, 0:cols, :], in0=src[:, :, :, 0:cols].rearrange("p k t h -> p k h t"),
+                scalar1=1.0, scalar2=0.0, op0=ALU.mult, op1=ALU.add,
             )
+
+        def r3g(pr):
+            if pr not in g3s:
+                g3s[pr] = work.tile([P, 2, H, PACK], BF16, name="g3", tag="g3", bufs=2, align_bytes=64)
+            regroup_pair(g3s[pr], xr[pr][:].rearrange("p k (t h) -> p k t h", t=PACK), G3)
+
+        def r2g(pr):
+            if pr not in g2s:
+                g2s[pr] = work.tile([P, 2, H, PACK], BF16, name="g2", tag="g2", bufs=1, align_bytes=64)
+            regroup_pair(g2s[pr], cs[pr], G2)
 
         g2s = {}
 
         def r2(c, engine, lo, hi):
-            if c not in g2s:
-                g2s[c] = work.tile([P, H, PACK], BF16, name="g2", tag="g2", bufs=2, align_bytes=64)
-            regroup(g2s[c], cs[c], lo, hi, engine)
+            pr = c // 2
+            if pr not in g2s:
+                tag = "g2" if pr < NP - 1 else "g2_last"
+                g2s[pr] = work.tile([P, 2, H, PACK], BF16, name="g2", tag=tag, bufs=1, align_bytes=64)
+            regroup(g2s[pr][:, c % 2], cs[pr][:, c % 2], lo, hi, engine)
 
         cq = {}
 
-        def q2(c):
-            q = work.tile([P, H], U32, name="cq", tag="cq", bufs=4, align_bytes=64)
-            s = work.tile([P, H], U8, name="cqs", tag="cqs", bufs=4, align_bytes=64)
-            quant(g2s[c][:].rearrange("p h t -> p (h t)"), q, s)
-            cq[c] = (q, s)
+        def q2(pr, half=None):
+            if pr not in cq:
+                q = work.tile([P, 2 * H], U32, name="cq", tag="cq", bufs=3, align_bytes=64)
+                s = work.tile([P, 2 * H], U8, name="cqs", tag="cqs", bufs=3, align_bytes=64)
+                cq[pr] = (q, s)
+            q, s = cq[pr]
+            if half is None:
+                quant(g2s[pr][:].rearrange("p k h t -> p (k h t)"), q[:], s[:])
+            else:
+                cols = slice(H * half, H * (half + 1))
+                quant(g2s[pr][:, half].rearrange("p h t -> p (h t)"), q[:, cols], s[:, cols])
 
         hebb = {}
 
-        def s2(c, ts):
-            q, s = xm[c]
-            rq, rs = cq[c]
+        def s2(c, ts=(0, 1, 2, 3)):
+            pr, half = c // 2, c % 2
+            q, s = xm[pr]
+            rq, rs = cq[pr]
+            rc = slice(H * half, H * (half + 1))
             for t in ts:
                 if c == 0:
                     hebb[t] = psum.tile([P, H], F32, name="hebb%d" % t, tag="hb%d" % t)
-                cols = slice(P * t, P * (t + 1))
+                cols = slice(H * half + P * t, H * half + P * (t + 1))
                 nc.tensor.matmul_mx(
                     out=hebb[t][:],
                     lhsT=q[:, cols].bitcast(FP8X4),
                     lhsT_scale=s[:, cols],
-                    rhs=rq[:].bitcast(FP8X4),
-                    rhs_scale=rs[:],
+                    rhs=rq[:, rc].bitcast(FP8X4),
+                    rhs_scale=rs[:, rc],
                     start=(c == 0),
                     stop=(c == NB - 1),
                 )
 
         gain_t = const.tile([P, 1], F32, name="gain_t")
-
         rs_sb = const.tile([P, 32], F32, name="rs_sb")
 
         def gain_a():
-            rs_ps = psum.tile([P, 32], F32, name="rs_ps", tag="tp", bufs=TP_BUFS)
+            rs_ps = psum.tile([P, 32], F32, name="rs_ps", tag="ps", bufs=4)
             nc.tensor.matmul(out=rs_ps[:], lhsT=ones_b[:], rhs=zb[:, 512:544], start=True, stop=True)
             nc.scalar.copy(out=rs_sb[:], in_=rs_ps[:])
 
@@ -232,15 +284,28 @@ def tile_neuroplasticitylayer_t_kernel(
         def fin():
             nw = const.tile([P, PACK, H], F32, name="nw")
             junk = const.tile([P, H], F32, name="junk")
-            acc = const.tile([P, PACK], F32, name="acc")
-            tot = psum.tile([P, 1], F32, name="tot", tag="ps", bufs=PS_BUFS)
-            for t in range(PACK):
+            junk_v = const.tile([P, HH], F32, name="junk_v")
+            acc_s = const.tile([P, 8], F32, name="acc_s")
+            acc_v = const.tile([P, 8], F32, name="acc_v")
+            tot = psum.tile([P, 1], F32, name="tot", tag="ps", bufs=4)
+            parts = [(0, 0, H), (1, 0, H), (2, 0, H), (3, 0, HH), (3, HH, H)]
+            for k, (t, lo, hi) in enumerate(parts):
                 nc.vector.scalar_tensor_tensor(
-                    out=nw[:, t, :], in0=hebb[t][:], scalar=gain_t[:, 0:1],
-                    in1=raw["p"][:, H * t : H * (t + 1)], op0=ALU.mult, op1=ALU.add,
+                    out=nw[:, t, lo:hi], in0=hebb[t][:, lo:hi], scalar=gain_t[:, 0:1],
+                    in1=raw["p"][:, H * t + lo : H * t + hi], op0=ALU.mult, op1=ALU.add,
                 )
-                nc.scalar.activation(out=junk[:], in_=nw[:, t, :], func=ACT.Square, accum_out=acc[:, t : t + 1])
-                nc.tensor.matmul(out=tot[:], lhsT=ones_f[:], rhs=acc[:, t : t + 1], start=(t == 0), stop=(t == PACK - 1))
+                if k < len(parts) - 1:
+                    nc.scalar.activation(
+                        out=junk[:, lo:hi], in_=nw[:, t, lo:hi], func=ACT.Square, accum_out=acc_s[:, k : k + 1]
+                    )
+                    part = acc_s[:, k : k + 1]
+                else:
+                    nc.vector.scalar_tensor_tensor(
+                        out=junk_v[:], in0=nw[:, t, lo:hi], scalar=1.0, in1=nw[:, t, lo:hi],
+                        op0=ALU.mult, op1=ALU.mult, accum_out=acc_v[:, 0:1],
+                    )
+                    part = acc_v[:, 0:1]
+                nc.tensor.matmul(out=tot[:], lhsT=ones_f[:], rhs=part, start=(k == 0), stop=(k == len(parts) - 1))
             rinv = const.tile([P, 1], F32, name="rinv")
             rraw = const.tile([P, 1], F32, name="rraw")
             nc.scalar.activation(out=rraw[:], in_=tot[:], func=ACT.Abs_reciprocal_sqrt)
@@ -260,79 +325,130 @@ def tile_neuroplasticitylayer_t_kernel(
                 load("b")
         for key in list(range(1, NB)) + ["r"]:
             load(key)
-        r3(0, "v", 0, 512)
-        th(0, 0, "hb2")
-        th(0, 1, "hb3")
+
+        def t_pair(pr):
+            for key in (2 * pr, 2 * pr + 1):
+                for b in range(2):
+                    th(key, b)
+
+        def e_pair(pr):
+            for key in (2 * pr, 2 * pr + 1):
+                for b in range(2):
+                    eh(key, b, "s")
+
+        r3(0, "v", 0, H)
+        th(0, 0)
+        th(0, 1)
         eh(0, 0, "s")
         eh(0, 1, "v")
         th("f", 0, "hb0")
         th("f", 1, "hb1")
-        q3(0)
-        q1(0)
+        q3(0, 0)
+        q1(0, 0)
         eh("f", 0, "s")
         eh("f", 1, "s")
-        th("p", 0, "tp")
-        th("p", 1, "tp")
-        q1("f")
+        th("p", 0, "hb2")
+        th("p", 1, "hb3")
+        q1("w", 0)
         eh("p", 0, "s")
         eh("p", 1, "s")
         bias()
-        r3(1, "v", 0, 384)
-        q1("p")
-        th(1, 0, "hb2")
-        th(1, 1, "hb3")
-        s1mm(0, 0)
-        s1mm(0, 1)
-        r3(1, "v", 384, 512)
+        r3(1, "v", 0, V1)
+        q1("w", 1)
+        th(1, 0)
+        th(1, 1)
         eh(1, 0, "s")
         eh(1, 1, "s")
-        th(2, 0, "tp")
-        th(2, 1, "tp")
-        nc.gpsimd.tensor_scalar(
-            out=hold[:], in0=g3s[1][:, 511, 3:4], scalar1=1.0, scalar2=0.0, op0=ALU.mult, op1=ALU.add
-        )
-        r3(2, "g", 0, G3)
-        r3(2, "s", G3, 512)
-        for i in range(NB):
-            if i + 2 < NB:
-                eh(i + 2, 0, "s")
-                eh(i + 2, 1, "s")
-            badd(i, 0)
-            badd(i, 1)
-            s1mm(i, 2)
-            s1mm(i, 3)
-            if i == 0:
-                q1(1)
-            if i + 1 < NB - 1:
-                q3(i + 1)
-            if i + 3 < NB:
-                r3(i + 3, "g", 0, G3)
-                r3(i + 3, "s", G3, 512)
-            if i >= 1:
-                q2(i - 1)
-            if i >= 2:
-                s2(i - 2, (0, 1, 2, 3))
-            badd(i, 2)
-            badd(i, 3)
-            store(i)
-            if i < NB - 1:
-                r2(i, "g", 0, G2)
-                r2(i, "s", G2, 512)
-                s1mm(i + 1, 0)
-                s1mm(i + 1, 1)
+        th(2, 0)
+        th(2, 1)
+        eh(2, 0, "s")
+        eh(2, 1, "s")
+        r3(1, "v", V1, H)
+        for n in range(4):
+            mm(0, n)
+        hold = const.tile([P, 1], U32, name="hold")
+        for n in range(4):
+            badd(0, n)
+        q1(0, 1)
+        q3(0, 1)
+        r3(2, "s", G3, H)
+        th(3, 0)
+        th(3, 1)
+        eh(3, 0, "s")
+        eh(3, 1, "s")
+        for n in range(4):
+            mm(0, n + 4)
+        nc.gpsimd.tensor_copy(out=hold[:], in_=xm[0][0][:, 2 * H - 1 : 2 * H])
+        r3g(1)
+        r3(3, "s", G3, H)
+        for n in range(4, 8):
+            badd(0, n)
+        t_pair(2)
+        e_pair(2)
+        q1(1)
+        q3(1)
+
+        for k in range(1, NP - 1):
+            a, b = 2 * k, 2 * k + 1
+            for n in range(4):
+                mm(k, n)
+            for n in range(8):
+                badd(k, n)
+                if n + 4 < 8:
+                    mm(k, n + 4)
+            if k == 1:
+                nc.gpsimd.tensor_copy(out=hold[:], in_=xm[1][0][:, 2 * H - 1 : 2 * H])
+            r2g(k - 1)
+            r3g(k + 1)
+            for c in (a - 2, b - 2):
+                r2(c, "s", G2, H)
+            for c in (a + 2, b + 2):
+                r3(c, "s", G3, H)
+            if k >= 2:
+                s2(a - 4)
+            if k + 2 < NP:
+                t_pair(k + 2)
+                e_pair(k + 2)
+            if k >= 2:
+                s2(b - 4)
+            if k < NP - 2:
+                q1(k + 1)
+                q3(k + 1)
+                q2(k - 1)
             else:
-                r2(i, "v", 0, TV)
-                r2(i, "s", TV, 512)
-                gain_a()
-            if i + 2 < NB:
-                q1(i + 2)
-            elif i == NB - 2:
-                q3(NB - 1)
-            if i + 3 < NB:
-                th(i + 3, 0, "tp")
-                th(i + 3, 1, "tp")
-        s2(NB - 2, (0, 1, 2, 3))
-        q2(NB - 1)
+                q2(k - 1)
+                q1(k + 1)
+                s2(a - 2)
+                q3(k + 1)
+        k = NP - 1
+        a, b = 2 * k, 2 * k + 1
+        for n in range(4):
+            mm(k, n)
+        for c in (a - 2, b - 2):
+            r2(c, "s", G2, H)
+        r2g(k - 1)
+        for n in range(4):
+            badd(k, n)
+            mm(k, n + 4)
+        r2(a, "s", 0, H)
+        s2(b - 4)
+        q2(k - 1, 0)
+        s2(a - 2)
+        badd(k, 4)
+        badd(k, 5)
+        q2(k - 1, 1)
+        s2(b - 2)
+        badd(k, 6)
+        badd(k, 7)
+        r2(b, "v", 0, TV)
+        r2(b, "s", TV, 512)
+        gain_a()
+        q2(k, 0)
+        q2(k, 1)
         gain_b()
-        s2(NB - 1, (0, 1, 2, 3))
+        s2(a, (0, 1))
+        for t in range(PACK):
+            s2(b, (t,))
+            if t + 2 < PACK:
+                s2(a, (t + 2,))
         fin()

@@ -22,7 +22,9 @@ NP = NB // 2
 FLOPS = 3 * 2 * ROWS * H * H
 G2 = 184
 G3 = 184
+V0 = 320
 V1 = 128
+V2 = 384
 TV = 256
 
 
@@ -40,6 +42,8 @@ def tile_neuroplasticitylayer_t_kernel(
         work = ctx.enter_context(tc.tile_pool(name="work", bufs=2))
         psum = ctx.enter_context(tc.psum_pool(name="psum", bufs=1))
 
+        wz = const.tile([P, H], BF16, name="wz")
+        nc.vector.memset(wz[:], 0.0)
         zb = const.tile([P, 544], BF16, name="zb")
         nc.vector.memset(zb[:], 0.0)
         warm = const.tile([P, 1], F32, name="warm")
@@ -51,6 +55,11 @@ def tile_neuroplasticitylayer_t_kernel(
         nc.vector.memset(ones_f[:], 1.0)
         ident = const.tile([P, P], F32, name="ident")
         make_identity(nc, ident[:])
+
+        def warm_pe(n):
+            for k in range(n):
+                dump = psum.tile([P, H], F32, name="dump", tag="hb3")
+                nc.tensor.matmul(out=dump[:], lhsT=wz[:, 0:P], rhs=wz[:], start=True, stop=True)
 
         raw = {}
         raw["f"] = const.tile([P, PACK * H], BF16, name="wf_raw")
@@ -154,7 +163,7 @@ def tile_neuroplasticitylayer_t_kernel(
         def r3(c, engine, lo, hi):
             pr = c // 2
             if pr not in g3s:
-                g3s[pr] = work.tile([P, 2, H, PACK], BF16, name="g3", tag="g3", bufs=2, align_bytes=64)
+                g3s[pr] = work.tile([P, 2, H, PACK], BF16, name="g3", tag="g3", bufs=1, align_bytes=64)
             regroup(g3s[pr][:, c % 2], raw[c][:].rearrange("p (t h) -> p t h", t=PACK), lo, hi, engine)
 
         def q3(pr, half=None):
@@ -215,7 +224,7 @@ def tile_neuroplasticitylayer_t_kernel(
 
         def r3g(pr):
             if pr not in g3s:
-                g3s[pr] = work.tile([P, 2, H, PACK], BF16, name="g3", tag="g3", bufs=2, align_bytes=64)
+                g3s[pr] = work.tile([P, 2, H, PACK], BF16, name="g3", tag="g3", bufs=1, align_bytes=64)
             regroup_pair(g3s[pr], xr[pr][:].rearrange("p k (t h) -> p k t h", t=PACK), G3)
 
         def r2g(pr):
@@ -283,7 +292,7 @@ def tile_neuroplasticitylayer_t_kernel(
 
         def fin():
             nw = const.tile([P, PACK, H], F32, name="nw")
-            junk = const.tile([P, H], F32, name="junk")
+            junk = const.tile([P, PACK, H], F32, name="junk")
             junk_v = const.tile([P, HH], F32, name="junk_v")
             acc_s = const.tile([P, 8], F32, name="acc_s")
             acc_v = const.tile([P, 8], F32, name="acc_v")
@@ -296,7 +305,7 @@ def tile_neuroplasticitylayer_t_kernel(
                 )
                 if k < len(parts) - 1:
                     nc.scalar.activation(
-                        out=junk[:, lo:hi], in_=nw[:, t, lo:hi], func=ACT.Square, accum_out=acc_s[:, k : k + 1]
+                        out=junk[:, t, lo:hi], in_=nw[:, t, lo:hi], func=ACT.Square, accum_out=acc_s[:, k : k + 1]
                     )
                     part = acc_s[:, k : k + 1]
                 else:
@@ -336,13 +345,17 @@ def tile_neuroplasticitylayer_t_kernel(
                 for b in range(2):
                     eh(key, b, "s")
 
-        r3(0, "v", 0, H)
+        warm_pe(5)
+        r3(0, "v", 0, V0)
+        r3(0, "s", V0, H)
         th(0, 0)
         th(0, 1)
+        warm_pe(1)
         eh(0, 0, "s")
         eh(0, 1, "v")
         th("f", 0, "hb0")
         th("f", 1, "hb1")
+        warm_pe(1)
         q3(0, 0)
         q1(0, 0)
         eh("f", 0, "s")
@@ -359,26 +372,29 @@ def tile_neuroplasticitylayer_t_kernel(
         th(1, 1)
         eh(1, 0, "s")
         eh(1, 1, "s")
+        mm(0, 0)
+        mm(0, 1)
+        r3(1, "v", V1, V2)
         th(2, 0)
         th(2, 1)
         eh(2, 0, "s")
         eh(2, 1, "s")
-        r3(1, "v", V1, H)
-        for n in range(4):
-            mm(0, n)
-        hold = const.tile([P, 1], U32, name="hold")
-        for n in range(4):
-            badd(0, n)
+        r3(1, "s", V2, H)
+        badd(0, 0)
+        mm(0, 2)
+        badd(0, 1)
+        mm(0, 3)
         q1(0, 1)
+        badd(0, 2)
+        badd(0, 3)
         q3(0, 1)
-        r3(2, "s", G3, H)
         th(3, 0)
         th(3, 1)
         eh(3, 0, "s")
         eh(3, 1, "s")
+        r3(2, "s", G3, H)
         for n in range(4):
             mm(0, n + 4)
-        nc.gpsimd.tensor_copy(out=hold[:], in_=xm[0][0][:, 2 * H - 1 : 2 * H])
         r3g(1)
         r3(3, "s", G3, H)
         for n in range(4, 8):
@@ -396,25 +412,30 @@ def tile_neuroplasticitylayer_t_kernel(
                 badd(k, n)
                 if n + 4 < 8:
                     mm(k, n + 4)
-            if k == 1:
-                nc.gpsimd.tensor_copy(out=hold[:], in_=xm[1][0][:, 2 * H - 1 : 2 * H])
-            r2g(k - 1)
             r3g(k + 1)
+            r2g(k - 1)
             for c in (a - 2, b - 2):
                 r2(c, "s", G2, H)
             for c in (a + 2, b + 2):
                 r3(c, "s", G3, H)
+            if k + 2 < NP:
+                th(a + 4, 0)
+                th(a + 4, 1)
+                eh(a + 4, 0, "s")
+                eh(a + 4, 1, "s")
             if k >= 2:
                 s2(a - 4)
             if k + 2 < NP:
-                t_pair(k + 2)
-                e_pair(k + 2)
+                th(b + 4, 0)
+                th(b + 4, 1)
+                eh(b + 4, 0, "s")
+                eh(b + 4, 1, "s")
             if k >= 2:
                 s2(b - 4)
             if k < NP - 2:
                 q1(k + 1)
-                q3(k + 1)
                 q2(k - 1)
+                q3(k + 1)
             else:
                 q2(k - 1)
                 q1(k + 1)

@@ -22,6 +22,7 @@ NP = NB // 2
 FLOPS = 3 * 2 * ROWS * H * H
 G2 = 184
 G3 = 184
+GT = 96
 V0 = 320
 V1 = 128
 V2 = 384
@@ -227,10 +228,10 @@ def tile_neuroplasticitylayer_t_kernel(
                 g3s[pr] = work.tile([P, 2, H, PACK], BF16, name="g3", tag="g3", bufs=1, align_bytes=64)
             regroup_pair(g3s[pr], xr[pr][:].rearrange("p k (t h) -> p k t h", t=PACK), G3)
 
-        def r2g(pr):
+        def r2g(pr, cols=G2):
             if pr not in g2s:
                 g2s[pr] = work.tile([P, 2, H, PACK], BF16, name="g2", tag="g2", bufs=1, align_bytes=64)
-            regroup_pair(g2s[pr], cs[pr], G2)
+            regroup_pair(g2s[pr], cs[pr], cols)
 
         g2s = {}
 
@@ -443,11 +444,13 @@ def tile_neuroplasticitylayer_t_kernel(
                 q3(k + 1)
         k = NP - 1
         a, b = 2 * k, 2 * k + 1
+        hold = const.tile([P, 1], U32, name="hold")
+        nc.gpsimd.tensor_copy(out=hold[:], in_=xm[k][0][:, 2 * H - 1 : 2 * H])
         for n in range(4):
             mm(k, n)
         for c in (a - 2, b - 2):
-            r2(c, "s", G2, H)
-        r2g(k - 1)
+            r2(c, "s", GT, H)
+        r2g(k - 1, GT)
         for n in range(4):
             badd(k, n)
             mm(k, n + 4)

@@ -401,6 +401,7 @@ def tile_neuroplasticitylayer_t_kernel(
         for n in range(4, 8):
             badd(0, n)
         t_pair(2)
+        warm_pe(2)
         e_pair(2)
         q1(1)
         q3(1)
@@ -426,6 +427,8 @@ def tile_neuroplasticitylayer_t_kernel(
                 eh(a + 4, 1, "s")
             if k >= 2:
                 s2(a - 4)
+            else:
+                warm_pe(2)
             if k + 2 < NP:
                 th(b + 4, 0)
                 th(b + 4, 1)
@@ -433,6 +436,8 @@ def tile_neuroplasticitylayer_t_kernel(
                 eh(b + 4, 1, "s")
             if k >= 2:
                 s2(b - 4)
+            else:
+                warm_pe(2)
             if k < NP - 2:
                 q1(k + 1)
                 q2(k - 1)

@@ -420,24 +420,15 @@ def tile_neuroplasticitylayer_t_kernel(
                 r2(c, "s", G2, H)
             for c in (a + 2, b + 2):
                 r3(c, "s", G3, H)
-            if k + 2 < NP:
-                th(a + 4, 0)
-                th(a + 4, 1)
-                eh(a + 4, 0, "s")
-                eh(a + 4, 1, "s")
             if k >= 2:
                 s2(a - 4)
-            else:
-                warm_pe(2)
             if k + 2 < NP:
-                th(b + 4, 0)
-                th(b + 4, 1)
-                eh(b + 4, 0, "s")
-                eh(b + 4, 1, "s")
+                t_pair(k + 2)
+                e_pair(k + 2)
             if k >= 2:
                 s2(b - 4)
             else:
-                warm_pe(2)
+                warm_pe(4)
             if k < NP - 2:
                 q1(k + 1)
                 q2(k - 1)

from contextlib import ExitStack

import concourse.mybir as mybir
from concourse.masks import make_identity

F32 = mybir.dt.float32
BF16 = mybir.dt.bfloat16
U32 = mybir.dt.uint32
U8 = mybir.dt.uint8
FP8X4 = mybir.dt.float8_e4m3fn_x4
ALU = mybir.AluOpType
ACT = mybir.ActivationFunctionType

P = 128
H = 512
HH = H // 2
ROWS = 6144
PACK = 4
BLK = P * PACK
NB = ROWS // BLK
NP = NB // 2
FLOPS = 3 * 2 * ROWS * H * H
G2 = 184
G3 = 184
GT = 96
V0 = 320
V1 = 128
V2 = 384
TV = 256


def tile_neuroplasticitylayer_t_kernel(
    tc, x, plastic_weights, plasticity_rate, fixed_w, fixed_b, hebbian_strength, out_0, out_1
):
    nc = tc.nc
    xf = x.flatten_outer_dims()
    of = out_0.flatten_outer_dims()

    with ExitStack() as ctx:
        ctx.enter_context(tc.manual_schedule())
        const = ctx.enter_context(tc.tile_pool(name="const", bufs=1))
        xpool = ctx.enter_context(tc.tile_pool(name="xpool", bufs=1))
        work = ctx.enter_context(tc.tile_pool(name="work", bufs=2))
        psum = ctx.enter_context(tc.psum_pool(name="psum", bufs=1))

        wz = const.tile([P, H], BF16, name="wz")
        nc.vector.memset(wz[:], 0.0)
        zb = const.tile([P, 544], BF16, name="zb")
        nc.vector.memset(zb[:], 0.0)
        warm = const.tile([P, 1], F32, name="warm")
        nc.vector.memset(warm[:], 1.0)
        nc.scalar.activation(out=warm[:], in_=warm[:], func=ACT.Abs_reciprocal_sqrt)
        ones_b = const.tile([P, P], BF16, name="ones_b")
        nc.vector.memset(ones_b[:], 1.0)
        ones_f = const.tile([P, P], F32, name="ones_f")
        nc.vector.memset(ones_f[:], 1.0)
        ident = const.tile([P, P], F32, name="ident")
        make_identity(nc, ident[:])

        def warm_pe(n):
            for k in range(n):
                dump = psum.tile([P, H], F32, name="dump", tag="hb3")
                nc.tensor.matmul(out=dump[:], lhsT=wz[:, 0:P], rhs=wz[:], start=True, stop=True)

        raw = {}
        raw["f"] = const.tile([P, PACK * H], BF16, name="wf_raw")
        raw["p"] = const.tile([P, PACK * H], BF16, name="wp_raw")
        xr = {}
        for pr in range(NP):
            xr[pr] = xpool.tile([P, 2, PACK * H], BF16, name="x_sb%d" % pr)
            for half in range(2):
                raw[2 * pr + half] = xr[pr][:, half, :]
        w_dram = {"f": fixed_w, "p": plastic_weights}

        def load(key, half=None):
            a0, a1 = (0, PACK) if half is None else (2 * half, 2 * half + 2)
            if key == "b":
                nc.sync.dma_start(out=zb[0:1, 0:H], in_=fixed_b.unsqueeze(0))
            elif key == "r":
                nc.sync.dma_start(out=zb[0:1, 512:513], in_=plasticity_rate.unsqueeze(0))
                nc.sync.dma_start(out=zb[0:1, 528:529], in_=hebbian_strength.unsqueeze(0))
            elif key in w_dram:
                nc.sync.dma_start(
                    out=raw[key][:, H * a0 : H * a1].rearrange("r (a h) -> r a h", h=H),
                    in_=w_dram[key].rearrange("(a r) h -> r a h", r=P)[:, a0:a1, :],
                )
            else:
                nc.sync.dma_start(
                    out=raw[key][:, H * a0 : H * a1].rearrange("p (j h) -> p j h", h=H),
                    in_=xf[BLK * key : BLK * (key + 1), :].rearrange("(p j) h -> p j h", j=PACK)[:, a0:a1, :],
                )

        g1s = {}
        tps = {}

        def slot(key):
            if key in w_dram:
                return "w", 0 if key == "f" else 1
            return key // 2, key % 2

        def bank(tag):
            if tag is None:
                return psum.tile([P, 4, P], F32, name="ps", tag="ps", bufs=4)
            return psum.tile([P, 4, P], F32, name="tp", tag=tag)

        def th(key, b, tag=None):
            pr, half = slot(key)
            if pr not in g1s:
                g1s[pr] = work.tile([P, 2, PACK * H], BF16, name="g1", tag="g1", bufs=2, align_bytes=64)
            srcw = raw[key][:].bitcast(F32)
            tp = bank(tag)
            tps[(key, b)] = tp
            for jj in range(2):
                for u in range(2):
                    col = 256 * (2 * b + jj) + 128 * u
                    nc.tensor.transpose(tp[:, 2 * jj + u, :], srcw[:, col : col + P], ident[:])

        def eh(key, b, engine):
            pr, half = slot(key)
            gw = g1s[pr][:, half, :].bitcast(F32).rearrange("p (j r u) -> p j r u", j=PACK, u=2)
            src_view = tps[(key, b)][:].rearrange("p (jj u) r -> p jj r u", u=2)
            if engine == "v":
                nc.vector.tensor_copy(out=gw[:, 2 * b : 2 * b + 2, :, :], in_=src_view)
            else:
                nc.scalar.copy(out=gw[:, 2 * b : 2 * b + 2, :, :], in_=src_view)

        def quant(grouped, codes, scales):
            nc.vector.quantize_mx(out=codes.bitcast(FP8X4), scales=scales, in_=grouped)

        xq = {}

        def q1(pr, half=None):
            if pr not in xq:
                if pr == "w":
                    q = const.tile([P, 2 * H], U32, name="wq", align_bytes=64)
                    s = const.tile([P, 2 * H], U8, name="ws", align_bytes=64)
                else:
                    q = work.tile([P, 2 * H], U32, name="xq", tag="xq", bufs=2, align_bytes=64)
                    s = work.tile([P, 2 * H], U8, name="xs", tag="xs", bufs=2, align_bytes=64)
                xq[pr] = (q, s)
            q, s = xq[pr]
            if half is None:
                quant(g1s[pr][:].rearrange("p k n -> p (k n)"), q[:], s[:])
            else:
                cols = slice(H * half, H * (half + 1))
                quant(g1s[pr][:, half, :], q[:, cols], s[:, cols])

        def regroup(dst, src, lo, hi, engine):
            d = dst[:, lo:hi, :].rearrange("p (c i) t -> p c t i", i=4)
            s = src[:, :, lo:hi].rearrange("p t (c i) -> p c t i", i=4)
            if engine == "v":
                nc.vector.tensor_copy(out=d, in_=s)
            elif engine == "s":
                nc.scalar.copy(out=d, in_=s)
            else:
                nc.gpsimd.tensor_scalar(
                    out=dst[:, lo:hi, :], in0=src[:, :, lo:hi].rearrange("p t h -> p h t"),
                    scalar1=1.0, scalar2=0.0, op0=ALU.mult, op1=ALU.add,
                )

        xm = {}
        g3s = {}

        def r3(c, engine, lo, hi):
            pr = c // 2
            if pr not in g3s:
                g3s[pr] = work.tile([P, 2, H, PACK], BF16, name="g3", tag="g3", bufs=1, align_bytes=64)
            regroup(g3s[pr][:, c % 2], raw[c][:].rearrange("p (t h) -> p t h", t=PACK), lo, hi, engine)

        def q3(pr, half=None):
            if pr not in xm:
                q = xpool.tile([P, 2 * H], U32, name="xmq%d" % pr, align_bytes=64)
                s = xpool.tile([P, 2 * H], U8, name="xms%d" % pr, align_bytes=64)
                xm[pr] = (q, s)
            q, s = xm[pr]
            if half is None:
                quant(g3s[pr][:].rearrange("p k h t -> p (k h t)"), q[:], s[:])
            else:
                cols = slice(H * half, H * (half + 1))
                quant(g3s[pr][:, half].rearrange("p h t -> p (h t)"), q[:, cols], s[:, cols])

        cs = {}
        pss = {}
        bias_bc = const.tile([P, H], F32, name="bias_bc")

        def bias():
            bias_ps = psum.tile([P, H], F32, name="bias_ps", tag="hb0")
            nc.tensor.matmul(out=bias_ps[:], lhsT=ones_b[:], rhs=zb[:, 0:H], start=True, stop=True)
            nc.scalar.copy(out=bias_bc[:], in_=bias_ps[:])

        def mm(pr, n):
            ps = psum.tile([P, H], F32, name="ps", tag="ps", bufs=4)
            pss[(pr, n)] = ps
            q, s = xq[pr]
            wq, ws = xq["w"]
            cols = slice(P * n, P * (n + 1))
            for m in range(2):
                wc = slice(H * m, H * (m + 1))
                nc.tensor.matmul_mx(
                    out=ps[:],
                    lhsT=q[:, cols].bitcast(FP8X4),
                    lhsT_scale=s[:, cols],
                    rhs=wq[:, wc].bitcast(FP8X4),
                    rhs_scale=ws[:, wc],
                    start=(m == 0),
                    stop=(m == 1),
                )

        def badd(pr, n):
            if n == 0:
                cs[pr] = work.tile([P, 2, PACK, H], F32, name="cs", tag="cs", bufs=2)
            nc.vector.tensor_tensor(out=cs[pr][:, n // PACK, n % PACK, :], in0=pss[(pr, n)][:], in1=bias_bc[:], op=ALU.add)
            if n % PACK == PACK - 1:
                c = 2 * pr + n // PACK
                nc.sync.dma_start(
                    out=of[BLK * c : BLK * (c + 1), :].rearrange("(p j) o -> p (j o)", j=PACK),
                    in_=cs[pr][:, n // PACK].rearrange("p j o -> p (j o)"),
                )

        def regroup_pair(dst, src, cols):
            nc.gpsimd.tensor_scalar(
                out=dst[:, :, 0:cols, :], in0=src[:, :, :, 0:cols].rearrange("p k t h -> p k h t"),
                scalar1=1.0, scalar2=0.0, op0=ALU.mult, op1=ALU.add,
            )

        def r3g(pr):
            if pr not in g3s:
                g3s[pr] = work.tile([P, 2, H, PACK], BF16, name="g3", tag="g3", bufs=1, align_bytes=64)
            regroup_pair(g3s[pr], xr[pr][:].rearrange("p k (t h) -> p k t h", t=PACK), G3)

        def r2g(pr, cols=G2):
            if pr not in g2s:
                g2s[pr] = work.tile([P, 2, H, PACK], BF16, name="g2", tag="g2", bufs=1, align_bytes=64)
            regroup_pair(g2s[pr], cs[pr], cols)

        g2s = {}

        def r2(c, engine, lo, hi):
            pr = c // 2
            if pr not in g2s:
                tag = "g2" if pr < NP - 1 else "g2_last"
                g2s[pr] = work.tile([P, 2, H, PACK], BF16, name="g2", tag=tag, bufs=1, align_bytes=64)
            regroup(g2s[pr][:, c % 2], cs[pr][:, c % 2], lo, hi, engine)

        cq = {}

        def q2(pr, half=None):
            if pr not in cq:
                q = work.tile([P, 2 * H], U32, name="cq", tag="cq", bufs=3, align_bytes=64)
                s = work.tile([P, 2 * H], U8, name="cqs", tag="cqs", bufs=3, align_bytes=64)
                cq[pr] = (q, s)
            q, s = cq[pr]
            if half is None:
                quant(g2s[pr][:].rearrange("p k h t -> p (k h t)"), q[:], s[:])
            else:
                cols = slice(H * half, H * (half + 1))
                quant(g2s[pr][:, half].rearrange("p h t -> p (h t)"), q[:, cols], s[:, cols])

        hebb = {}

        def s2(c, ts=(0, 1, 2, 3)):
            pr, half = c // 2, c % 2
            q, s = xm[pr]
            rq, rs = cq[pr]
            rc = slice(H * half, H * (half + 1))
            for t in ts:
                if c == 0:
                    hebb[t] = psum.tile([P, H], F32, name="hebb%d" % t, tag="hb%d" % t)
                cols = slice(H * half + P * t, H * half + P * (t + 1))
                nc.tensor.matmul_mx(
                    out=hebb[t][:],
                    lhsT=q[:, cols].bitcast(FP8X4),
                    lhsT_scale=s[:, cols],
                    rhs=rq[:, rc].bitcast(FP8X4),
                    rhs_scale=rs[:, rc],
                    start=(c == 0),
                    stop=(c == NB - 1),
                )

        gain_t = const.tile([P, 1], F32, name="gain_t")
        rs_sb = const.tile([P, 32], F32, name="rs_sb")

        def gain_a():
            rs_ps = psum.tile([P, 32], F32, name="rs_ps", tag="ps", bufs=4)
            nc.tensor.matmul(out=rs_ps[:], lhsT=ones_b[:], rhs=zb[:, 512:544], start=True, stop=True)
            nc.scalar.copy(out=rs_sb[:], in_=rs_ps[:])

        def gain_b():
            nc.vector.scalar_tensor_tensor(
                out=gain_t[:], in0=rs_sb[:, 0:1], scalar=1.0 / ROWS, in1=rs_sb[:, 16:17],
                op0=ALU.mult, op1=ALU.mult,
            )

        def fin():
            nw = const.tile([P, PACK, H], F32, name="nw")
            junk = const.tile([P, PACK, H], F32, name="junk")
            junk_v = const.tile([P, HH], F32, name="junk_v")
            acc_s = const.tile([P, 8], F32, name="acc_s")
            acc_v = const.tile([P, 8], F32, name="acc_v")
            tot = psum.tile([P, 1], F32, name="tot", tag="ps", bufs=4)
            parts = [(0, 0, H), (1, 0, H), (2, 0, H), (3, 0, HH), (3, HH, H)]
            for k, (t, lo, hi) in enumerate(parts):
                nc.vector.scalar_tensor_tensor(
                    out=nw[:, t, lo:hi], in0=hebb[t][:, lo:hi], scalar=gain_t[:, 0:1],
                    in1=raw["p"][:, H * t + lo : H * t + hi], op0=ALU.mult, op1=ALU.add,
                )
                if k < len(parts) - 1:
                    nc.scalar.activation(
                        out=junk[:, t, lo:hi], in_=nw[:, t, lo:hi], func=ACT.Square, accum_out=acc_s[:, k : k + 1]
                    )
                    part = acc_s[:, k : k + 1]
                else:
                    nc.vector.scalar_tensor_tensor(
                        out=junk_v[:], in0=nw[:, t, lo:hi], scalar=1.0, in1=nw[:, t, lo:hi],
                        op0=ALU.mult, op1=ALU.mult, accum_out=acc_v[:, 0:1],
                    )
                    part = acc_v[:, 0:1]
                nc.tensor.matmul(out=tot[:], lhsT=ones_f[:], rhs=part, start=(k == 0), stop=(k == len(parts) - 1))
            rinv = const.tile([P, 1], F32, name="rinv")
            rraw = const.tile([P, 1], F32, name="rraw")
            nc.scalar.activation(out=rraw[:], in_=tot[:], func=ACT.Abs_reciprocal_sqrt)
            nc.vector.tensor_scalar_min(out=rinv[:], in0=rraw[:], scalar1=1.0)
            res = const.tile([P, PACK, H], F32, name="res")
            o1 = out_1.rearrange("(t p) j -> p t j", p=P)
            nc.scalar.activation(out=res[:, 0, :], in_=nw[:, 0, :], func=ACT.Copy, scale=rinv[:, 0:1])
            for t in (1, 2, 0, 3):
                if t > 0:
                    nc.vector.tensor_scalar_mul(out=res[:, t, :], in0=nw[:, t, :], scalar1=rinv[:, 0:1])
                nc.sync.dma_start(out=o1[:, t, :], in_=res[:, t, :])

        for key in (0, "f", "p"):
            load(key, 0)
            load(key, 1)
            if key == "f":
                load("b")
        for key in list(range(1, NB)) + ["r"]:
            load(key)

        def t_pair(pr):
            for key in (2 * pr, 2 * pr + 1):
                for b in range(2):
                    th(key, b)

        def e_pair(pr):
            for key in (2 * pr, 2 * pr + 1):
                for b in range(2):
                    eh(key, b, "s")

        warm_pe(5)
        r3(0, "v", 0, V0)
        r3(0, "s", V0, H)
        th(0, 0)
        th(0, 1)
        warm_pe(1)
        eh(0, 0, "s")
        eh(0, 1, "v")
        th("f", 0, "hb0")
        th("f", 1, "hb1")
        warm_pe(1)
        q3(0, 0)
        q1(0, 0)
        eh("f", 0, "s")
        eh("f", 1, "s")
        th("p", 0, "hb2")
        th("p", 1, "hb3")
        q1("w", 0)
        eh("p", 0, "s")
        eh("p", 1, "s")
        bias()
        r3(1, "v", 0, V1)
        q1("w", 1)
        th(1, 0)
        th(1, 1)
        eh(1, 0, "s")
        eh(1, 1, "s")
        mm(0, 0)
        mm(0, 1)
        r3(1, "v", V1, V2)
        th(2, 0)
        th(2, 1)
        eh(2, 0, "s")
        eh(2, 1, "s")
        r3(1, "s", V2, H)
        badd(0, 0)
        mm(0, 2)
        badd(0, 1)
        mm(0, 3)
        q1(0, 1)
        badd(0, 2)
        badd(0, 3)
        q3(0, 1)
        th(3, 0)
        th(3, 1)
        eh(3, 0, "s")
        eh(3, 1, "s")
        r3(2, "s", G3, H)
        for n in range(4):
            mm(0, n + 4)
        r3g(1)
        r3(3, "s", G3, H)
        for n in range(4, 8):
            badd(0, n)
        t_pair(2)
        warm_pe(2)
        e_pair(2)
        q1(1)
        q3(1)

        for k in range(1, NP - 1):
            a, b = 2 * k, 2 * k + 1
            for n in range(4):
                mm(k, n)
            for n in range(8):
                badd(k, n)
                if n + 4 < 8:
                    mm(k, n + 4)
            r3g(k + 1)
            r2g(k - 1)
            for c in (a - 2, b - 2):
                r2(c, "s", G2, H)
            for c in (a + 2, b + 2):
                r3(c, "s", G3, H)
            if k >= 2:
                s2(a - 4)
            if k + 2 < NP:
                t_pair(k + 2)
                e_pair(k + 2)
            if k >= 2:
                s2(b - 4)
            else:
                warm_pe(4)
            if k < NP - 2:
                q1(k + 1)
                q2(k - 1)
                q3(k + 1)
            else:
                q2(k - 1)
                q1(k + 1)
                s2(a - 2)
                q3(k + 1)
        k = NP - 1
        a, b = 2 * k, 2 * k + 1
        hold = const.tile([P, 1], U32, name="hold")
        nc.gpsimd.tensor_copy(out=hold[:], in_=xm[k][0][:, 2 * H - 1 : 2 * H])
        for n in range(4):
            mm(k, n)
        for c in (a - 2, b - 2):
            r2(c, "s", GT, H)
        r2g(k - 1, GT)
        for n in range(4):
            badd(k, n)
            mm(k, n + 4)
        r2(a, "s", 0, H)
        s2(b - 4)
        q2(k - 1, 0)
        s2(a - 2)
        badd(k, 4)
        badd(k, 5)
        q2(k - 1, 1)
        s2(b - 2)
        badd(k, 6)
        badd(k, 7)
        r2(b, "v", 0, TV)
        r2(b, "s", TV, 512)
        gain_a()
        q2(k, 0)
        q2(k, 1)
        gain_b()
        s2(a, (0, 1))
        for t in range(PACK):
            s2(b, (t,))
            if t + 2 < PACK:
                s2(a, (t + 2,))
        fin()
